import numpy as np
import ml_dtypes


def mxq(x, axis, fmt="e4m3"):
    dtype, down = {"e4m3": (ml_dtypes.float8_e4m3fn, 7), "e5m2": (ml_dtypes.float8_e5m2, 14)}[fmt]
    v = np.moveaxis(np.asarray(x, np.float32).astype(ml_dtypes.bfloat16).astype(np.float64), axis, -1)
    blocks = v.reshape(v.shape[:-1] + (-1, 32))
    amax = np.abs(blocks).max(-1, keepdims=True)
    byte = np.maximum(np.where(amax > 0, np.frexp(amax)[1] - 1 + 127, 0) - down, 1)
    scale = np.exp2(byte - 127.0)
    codes = (blocks / scale).astype(np.float32).astype(dtype).astype(np.float64)
    return np.moveaxis((codes * scale).reshape(v.shape), -1, axis)


WIDE = False


def mx_kscale(k):
    if not WIDE:
        return np.ones(k)
    levels = np.array([20, -20, 10, -10, 0])
    a = np.random.permutation(np.resize(levels, k // 512 * 4)).reshape(k // 512, 4)
    idx = np.arange(k)
    return np.exp2(a[idx // 512, idx % 128 // 32])


BF16 = ml_dtypes.bfloat16


def bf(x):
    return np.asarray(x, np.float32).astype(BF16)


def f64(x):
    return np.asarray(x).astype(np.float64)


NUM_PLANES = 80
BOARD = 8 * 8
IN_DIM = NUM_PLANES * BOARD
OUT_DIM = 2048
B = 512


def setup_inputs():
    u = mx_kscale(OUT_DIM)
    x = np.random.standard_normal((B, NUM_PLANES, 8, 8))
    rows = np.random.randint(0, IN_DIM, size=OUT_DIM)
    m = np.random.standard_normal((IN_DIM, OUT_DIM)) * 0.01
    m[rows, np.arange(OUT_DIM)] += 1.0
    g = np.random.standard_normal((B, OUT_DIM)) * np.exp2(np.random.randint(-12, 1, (B, 1))) * 8.0 * u
    return {"x": bf(x), "fc1": bf(m / u[None, :]), "grad_out": bf(g)}


def reference(x, fc1, grad_out):
    gh = mxq(f64(grad_out), 1, "e5m2") @ mxq(f64(fc1), 1, "e4m3").T
    return gh.reshape(-1, NUM_PLANES, 8, 8)

@@ -1,0 +1,185 @@
+from contextlib import ExitStack
+
+import concourse.mybir as mybir
+from concourse.masks import make_identity
+
+F32 = mybir.dt.float32
+BF16 = mybir.dt.bfloat16
+U32 = mybir.dt.uint32
+U8 = mybir.dt.uint8
+E4X4 = mybir.dt.float8_e4m3fn_x4
+E5X4 = mybir.dt.float8_e5m2_x4
+
+P = 128
+B = 512
+IN_DIM = 5120
+K = 2048
+NJ = IN_DIM // 512
+NG = K // 512
+
+FLOPS = 2 * B * IN_DIM * K
+BYTES = IN_DIM * K * 2 + B * K * 2 + B * IN_DIM * 4
+
+
+def tile_applypolicymap_kernel(tc, x, fc1, grad_out, out):
+    nc = tc.nc
+    out2d = out.rearrange("b c h w -> b (c h w)")
+
+    with ExitStack() as ctx:
+        const = ctx.enter_context(tc.tile_pool(name="const", bufs=1))
+        quarter = ctx.enter_context(tc.tile_pool(name="quarter", bufs=8))
+        half = ctx.enter_context(tc.tile_pool(name="half", bufs=4))
+        whole = ctx.enter_context(tc.tile_pool(name="whole", bufs=4))
+        gpool = ctx.enter_context(tc.tile_pool(name="grouped", bufs=6))
+        wq = ctx.enter_context(tc.tile_pool(name="wq", bufs=12))
+        gq = ctx.enter_context(tc.tile_pool(name="gq", bufs=4))
+        spool = ctx.enter_context(tc.tile_pool(name="stage", bufs=8))
+        psum_t = ctx.enter_context(tc.psum_pool(name="psum_t", bufs=4))
+        psum_o = ctx.enter_context(tc.psum_pool(name="psum_o", bufs=4))
+        ctx.enter_context(tc.manual_schedule())
+
+        ident = const.tile([P, P], F32, name="ident")
+        make_identity(nc, ident[:])
+
+        def load(pool, src, row0, k0, klen, label):
+            raw = pool.tile([P, 4 * klen], BF16, name=label, tag=label)
+            nc.sync.dma_start(
+                out=raw[:].rearrange("p (r k) -> p r k", r=4),
+                in_=src[row0 : row0 + 512, k0 : k0 + klen].rearrange("(r p) k -> p r k", p=P),
+            )
+            return raw
+
+        def chunk(raw, klen, g_local, fmt, pool, label):
+            return {
+                "words": raw[:].bitcast(F32),
+                "rstride": klen // 2,
+                "goff": 256 * g_local,
+                "fmt": fmt,
+                "pool": pool,
+                "label": label,
+            }
+
+        def transposes(c):
+            banks = []
+            for h in range(2):
+                bank = psum_t.tile([P, 512], F32, name="tb", tag="tb")
+                for rr in range(2):
+                    for u in range(2):
+                        off = (2 * h + rr) * c["rstride"] + c["goff"] + 128 * u
+                        col = (2 * rr + u) * 128
+                        nc.tensor.transpose(bank[:, col : col + 128], c["words"][:, off : off + 128], ident[:])
+                banks.append(bank)
+            c["banks"] = banks
+
+        def copies(c):
+            grouped = gpool.tile([P, 2048], BF16, name="grp", tag="grp", align_bytes=64)
+            gw = grouped[:].bitcast(F32)
+            for h in range(2):
+                dst = gw[:, 512 * h : 512 * h + 512].rearrange("p (r i u) -> p r i u", r=2, u=2)
+                src = c["banks"][h][:].rearrange("p (r u i) -> p r i u", r=2, u=2)
+                if h == 0:
+                    nc.scalar.copy(out=dst, in_=src)
+                else:
+                    nc.vector.tensor_copy(out=dst, in_=src)
+            c["grouped"] = grouped
+
+        def quantise(c):
+            codes = c["pool"].tile([P, 512], U32, name=c["label"] + "c", tag=c["label"] + "c", align_bytes=64)
+            scales = c["pool"].tile([P, 512], U8, name=c["label"] + "s", tag=c["label"] + "s", align_bytes=64)
+            nc.vector.quantize_mx(out=codes[:].bitcast(c["fmt"]), scales=scales[:], in_=c["grouped"][:])
+            c["codes"] = codes
+            c["scales"] = scales
+
+        def prepare(chunks):
+            for c in chunks:
+                transposes(c)
+            for c in chunks:
+                copies(c)
+            for c in chunks:
+                quantise(c)
+
+        def mx_pass(bank, gc, wc, bt, start, stop):
+            cols = slice(bt * P, (bt + 1) * P)
+            nc.tensor.matmul_mx(
+                out=bank[:],
+                lhsT=gc["codes"][:, cols].bitcast(E5X4),
+                lhsT_scale=gc["scales"][:, cols],
+                rhs=wc["codes"][:].bitcast(E4X4),
+                rhs_scale=wc["scales"][:],
+                start=start,
+                stop=stop,
+            )
+
+        def drain(banks, j, bt0, split):
+            stage = spool.tile([P, 1024], F32, name="st", tag="st")
+            for i in range(2):
+                nc.scalar.copy(out=stage[:, 512 * i : 512 * i + 512], in_=banks[i][:])
+                if split:
+                    r0 = (bt0 + i) * P
+                    nc.sync.dma_start(
+                        out=out2d[r0 : r0 + P, 512 * j : 512 * j + 512], in_=stage[:, 512 * i : 512 * i + 512]
+                    )
+            if not split:
+                nc.sync.dma_start(
+                    out=out2d[bt0 * P : (bt0 + 2) * P, 512 * j : 512 * j + 512].rearrange("(b p) c -> p b c", p=P),
+                    in_=stage[:].rearrange("p (b c) -> p b c", b=2),
+                )
+
+        def mx_run(gcs, wcs, j, bt0, split):
+            banks = []
+            for bt in (bt0, bt0 + 1):
+                bank = psum_o.tile([P, 512], F32, name="ob", tag="ob")
+                for g in range(NG):
+                    mx_pass(bank, gcs[g], wcs[g], bt, g == 0, g == NG - 1)
+                banks.append(bank)
+            drain(banks, j, bt0, split)
+
+        g_raw = []
+        w0_raw = []
+        for g in range(NG):
+            g_raw.append(load(quarter, grad_out, 0, 512 * g, 512, "q"))
+            w0_raw.append(load(quarter, fc1, 0, 512 * g, 512, "q"))
+        w_chunks = {}
+        for j in (1, 2):
+            cs = []
+            for hk in range(2):
+                raw = load(half, fc1, 512 * j, 1024 * hk, 1024, "h")
+                cs.extend([chunk(raw, 1024, gl, E4X4, wq, "w") for gl in range(2)])
+            w_chunks[j] = cs
+
+        def load_whole(j):
+            raw = load(whole, fc1, 512 * j, 0, K, "wj")
+            w_chunks[j] = [chunk(raw, K, g, E4X4, wq, "w") for g in range(NG)]
+
+        load_whole(3)
+        load_whole(4)
+
+        g_chunks = [chunk(g_raw[g], 512, 0, E5X4, gq, "g") for g in range(NG)]
+        w_chunks[0] = [chunk(w0_raw[g], 512, 0, E4X4, wq, "w") for g in range(NG)]
+        banks0 = [psum_o.tile([P, 512], F32, name="ob", tag="ob") for bt in range(4)]
+
+        def head_run(g):
+            for bt in range(4):
+                mx_pass(banks0[bt], g_chunks[g], w_chunks[0][g], bt, g == 0, g == NG - 1)
+
+        for g in range(NG):
+            prepare([g_chunks[g]])
+            prepare([w_chunks[0][g]])
+            if g >= 1:
+                head_run(g - 1)
+        prepare(w_chunks[1][0:2])
+        head_run(NG - 1)
+        drain(banks0[0:2], 0, 0, False)
+        drain(banks0[2:4], 0, 2, False)
+        prepare(w_chunks[1][2:4])
+
+        for j in range(1, NJ):
+            last = j == NJ - 1
+            if j + 4 < NJ:
+                load_whole(j + 4)
+            if not last:
+                prepare(w_chunks[j + 1][0:2])
+            mx_run(g_chunks, w_chunks[j], j, 0, False)
+            if not last:
+                prepare(w_chunks[j + 1][2:4])
+            mx_run(g_chunks, w_chunks[j], j, 2, last)

@@ -30,10 +30,10 @@ def tile_applypolicymap_kernel(tc, x, fc1, grad_out, out):
         quarter = ctx.enter_context(tc.tile_pool(name="quarter", bufs=8))
         half = ctx.enter_context(tc.tile_pool(name="half", bufs=4))
         whole = ctx.enter_context(tc.tile_pool(name="whole", bufs=4))
-        gpool = ctx.enter_context(tc.tile_pool(name="grouped", bufs=6))
-        wq = ctx.enter_context(tc.tile_pool(name="wq", bufs=12))
+        gpool = ctx.enter_context(tc.tile_pool(name="grouped", bufs=5))
+        wq = ctx.enter_context(tc.tile_pool(name="wq", bufs=10))
         gq = ctx.enter_context(tc.tile_pool(name="gq", bufs=4))
-        spool = ctx.enter_context(tc.tile_pool(name="stage", bufs=8))
+        spool = ctx.enter_context(tc.tile_pool(name="stage", bufs=5))
         psum_t = ctx.enter_context(tc.psum_pool(name="psum_t", bufs=4))
         psum_o = ctx.enter_context(tc.psum_pool(name="psum_o", bufs=4))
         ctx.enter_context(tc.manual_schedule())
@@ -110,29 +110,37 @@ def tile_applypolicymap_kernel(tc, x, fc1, grad_out, out):
                 stop=stop,
             )
 
-        def drain(banks, j, bt0, split):
-            stage = spool.tile([P, 1024], F32, name="st", tag="st")
+        stages = {}
+
+        def drain(banks, j, bt0):
+            paired = j < NJ - 2
+            width = 1024 if paired else 512
+            c0 = 512 * (j % 2) if paired else 0
+            key = (j // 2 if paired else j + NJ, bt0)
+            if key not in stages:
+                stages[key] = spool.tile([P, 2 * width], F32, name="st", tag="st")
+            stage = stages[key][:].rearrange("p (b c) -> p b c", b=2)
+            last = j == NJ - 1 and bt0 == 2
             for i in range(2):
-                nc.scalar.copy(out=stage[:, 512 * i : 512 * i + 512], in_=banks[i][:])
-                if split:
+                nc.scalar.copy(out=stage[:, i, c0 : c0 + 512], in_=banks[i][:])
+                if last:
                     r0 = (bt0 + i) * P
-                    nc.sync.dma_start(
-                        out=out2d[r0 : r0 + P, 512 * j : 512 * j + 512], in_=stage[:, 512 * i : 512 * i + 512]
-                    )
-            if not split:
+                    nc.sync.dma_start(out=out2d[r0 : r0 + P, 512 * j : 512 * j + 512], in_=stage[:, i, :])
+            if not last and (not paired or j % 2 == 1):
+                col0 = 512 * j + 512 - width
                 nc.sync.dma_start(
-                    out=out2d[bt0 * P : (bt0 + 2) * P, 512 * j : 512 * j + 512].rearrange("(b p) c -> p b c", p=P),
-                    in_=stage[:].rearrange("p (b c) -> p b c", b=2),
+                    out=out2d[bt0 * P : (bt0 + 2) * P, col0 : col0 + width].rearrange("(b p) c -> p b c", p=P),
+                    in_=stage,
                 )
 
-        def mx_run(gcs, wcs, j, bt0, split):
+        def mx_run(gcs, wcs, j, bt0):
             banks = []
             for bt in (bt0, bt0 + 1):
                 bank = psum_o.tile([P, 512], F32, name="ob", tag="ob")
                 for g in range(NG):
                     mx_pass(bank, gcs[g], wcs[g], bt, g == 0, g == NG - 1)
                 banks.append(bank)
-            drain(banks, j, bt0, split)
+            drain(banks, j, bt0)
 
         g_raw = []
         w0_raw = []
@@ -169,17 +177,19 @@ def tile_applypolicymap_kernel(tc, x, fc1, grad_out, out):
                 head_run(g - 1)
         prepare(w_chunks[1][0:2])
         head_run(NG - 1)
-        drain(banks0[0:2], 0, 0, False)
-        drain(banks0[2:4], 0, 2, False)
+        drain(banks0[0:2], 0, 0)
+        drain(banks0[2:4], 0, 2)
         prepare(w_chunks[1][2:4])
 
         for j in range(1, NJ):
             last = j == NJ - 1
-            if j + 4 < NJ:
-                load_whole(j + 4)
             if not last:
                 prepare(w_chunks[j + 1][0:2])
-            mx_run(g_chunks, w_chunks[j], j, 0, False)
+            mx_run(g_chunks, w_chunks[j], j, 0)
             if not last:
                 prepare(w_chunks[j + 1][2:4])
-            mx_run(g_chunks, w_chunks[j], j, 2, last)
+            mx_run(g_chunks, w_chunks[j], j, 2)
+            if j % 2 == 1:
+                for jn in (j + 4, j + 5):
+                    if jn < NJ:
+                        load_whole(jn)

@@ -34,8 +34,7 @@ def tile_applypolicymap_kernel(tc, x, fc1, grad_out, out):
         wq = ctx.enter_context(tc.tile_pool(name="wq", bufs=10))
         gq = ctx.enter_context(tc.tile_pool(name="gq", bufs=4))
         spool = ctx.enter_context(tc.tile_pool(name="stage", bufs=5))
-        psum_t = ctx.enter_context(tc.psum_pool(name="psum_t", bufs=4))
-        psum_o = ctx.enter_context(tc.psum_pool(name="psum_o", bufs=4))
+        psum = ctx.enter_context(tc.psum_pool(name="psum", bufs=8))
         ctx.enter_context(tc.manual_schedule())
 
         ident = const.tile([P, P], F32, name="ident")
@@ -62,7 +61,7 @@ def tile_applypolicymap_kernel(tc, x, fc1, grad_out, out):
         def transposes(c):
             banks = []
             for h in range(2):
-                bank = psum_t.tile([P, 512], F32, name="tb", tag="tb")
+                bank = psum.tile([P, 512], F32, name="bank", tag="bank")
                 for rr in range(2):
                     for u in range(2):
                         off = (2 * h + rr) * c["rstride"] + c["goff"] + 128 * u
@@ -136,7 +135,7 @@ def tile_applypolicymap_kernel(tc, x, fc1, grad_out, out):
         def mx_run(gcs, wcs, j, bt0):
             banks = []
             for bt in (bt0, bt0 + 1):
-                bank = psum_o.tile([P, 512], F32, name="ob", tag="ob")
+                bank = psum.tile([P, 512], F32, name="bank", tag="bank")
                 for g in range(NG):
                     mx_pass(bank, gcs[g], wcs[g], bt, g == 0, g == NG - 1)
                 banks.append(bank)
@@ -164,7 +163,7 @@ def tile_applypolicymap_kernel(tc, x, fc1, grad_out, out):
 
         g_chunks = [chunk(g_raw[g], 512, 0, E5X4, gq, "g") for g in range(NG)]
         w_chunks[0] = [chunk(w0_raw[g], 512, 0, E4X4, wq, "w") for g in range(NG)]
-        banks0 = [psum_o.tile([P, 512], F32, name="ob", tag="ob") for bt in range(4)]
+        banks0 = [psum.tile([P, 512], F32, name="bank", tag="bank") for bt in range(4)]
 
         def head_run(g):
             for bt in range(4):
@@ -183,10 +182,11 @@ def tile_applypolicymap_kernel(tc, x, fc1, grad_out, out):
 
         for j in range(1, NJ):
             last = j == NJ - 1
+            long_runs = j >= 3
             if not last:
-                prepare(w_chunks[j + 1][0:2])
+                prepare(w_chunks[j + 1] if long_runs else w_chunks[j + 1][0:2])
             mx_run(g_chunks, w_chunks[j], j, 0)
-            if not last:
+            if not last and not long_runs:
                 prepare(w_chunks[j + 1][2:4])
             mx_run(g_chunks, w_chunks[j], j, 2)
             if j % 2 == 1:

@@ -14,6 +14,7 @@ P = 128
 B = 512
 IN_DIM = 5120
 K = 2048
+KW = K // 2
 NJ = IN_DIM // 512
 NG = K // 512
 
@@ -27,86 +28,92 @@ def tile_applypolicymap_kernel(tc, x, fc1, grad_out, out):
 
     with ExitStack() as ctx:
         const = ctx.enter_context(tc.tile_pool(name="const", bufs=1))
-        quarter = ctx.enter_context(tc.tile_pool(name="quarter", bufs=8))
-        half = ctx.enter_context(tc.tile_pool(name="half", bufs=4))
-        whole = ctx.enter_context(tc.tile_pool(name="whole", bufs=4))
-        gpool = ctx.enter_context(tc.tile_pool(name="grouped", bufs=5))
+        slices = ctx.enter_context(tc.tile_pool(name="slices", bufs=8))
+        halves = ctx.enter_context(tc.tile_pool(name="halves", bufs=8))
+        gpool = ctx.enter_context(tc.tile_pool(name="grouped", bufs=4))
         wq = ctx.enter_context(tc.tile_pool(name="wq", bufs=10))
         gq = ctx.enter_context(tc.tile_pool(name="gq", bufs=4))
-        spool = ctx.enter_context(tc.tile_pool(name="stage", bufs=5))
+        spool = ctx.enter_context(tc.tile_pool(name="stage", bufs=7))
         psum = ctx.enter_context(tc.psum_pool(name="psum", bufs=8))
         ctx.enter_context(tc.manual_schedule())
 
         ident = const.tile([P, P], F32, name="ident")
         make_identity(nc, ident[:])
 
-        def load(pool, src, row0, k0, klen, label):
-            raw = pool.tile([P, 4 * klen], BF16, name=label, tag=label)
-            nc.sync.dma_start(
-                out=raw[:].rearrange("p (r k) -> p r k", r=4),
-                in_=src[row0 : row0 + 512, k0 : k0 + klen].rearrange("(r p) k -> p r k", p=P),
-            )
-            return raw
-
-        def chunk(raw, klen, g_local, fmt, pool, label):
+        def new_block(src, row0, fmt, pool, label):
             return {
-                "words": raw[:].bitcast(F32),
-                "rstride": klen // 2,
-                "goff": 256 * g_local,
+                "rows": src[row0 : row0 + 512, :].rearrange("(r p) k -> p r k", p=P),
                 "fmt": fmt,
                 "pool": pool,
                 "label": label,
+                "words": {},
+                "banks": {},
             }
 
-        def transposes(c):
-            banks = []
-            for h in range(2):
-                bank = psum.tile([P, 512], F32, name="bank", tag="bank")
-                for rr in range(2):
-                    for u in range(2):
-                        off = (2 * h + rr) * c["rstride"] + c["goff"] + 128 * u
-                        col = (2 * rr + u) * 128
-                        nc.tensor.transpose(bank[:, col : col + 128], c["words"][:, off : off + 128], ident[:])
-                banks.append(bank)
-            c["banks"] = banks
+        def load(blk, pool, r0, nr, label):
+            raw = pool.tile([P, nr * K], BF16, name=label, tag=label)
+            nc.sync.dma_start(out=raw[:].rearrange("p (r k) -> p r k", r=nr), in_=blk["rows"][:, r0 : r0 + nr, :])
+            for i in range(nr):
+                blk["words"][r0 + i] = raw[:].bitcast(F32)[:, i * KW : (i + 1) * KW]
 
-        def copies(c):
-            grouped = gpool.tile([P, 2048], BF16, name="grp", tag="grp", align_bytes=64)
-            gw = grouped[:].bitcast(F32)
-            for h in range(2):
-                dst = gw[:, 512 * h : 512 * h + 512].rearrange("p (r i u) -> p r i u", r=2, u=2)
-                src = c["banks"][h][:].rearrange("p (r u i) -> p r i u", r=2, u=2)
-                if h == 0:
+        def transposes(blk, r):
+            for gp in range(2):
+                bank = psum.tile([P, 512], F32, name="bank", tag="bank")
+                for g2 in range(2):
+                    for u in range(2):
+                        off = (2 * gp + g2) * 256 + 128 * u
+                        col = (2 * g2 + u) * 128
+                        nc.tensor.transpose(bank[:, col : col + 128], blk["words"][r][:, off : off + 128], ident[:])
+                blk["banks"][(r, gp)] = bank
+
+        def open_block(blk):
+            blk["grouped"] = [gpool.tile([P, 4096], BF16, name="grp", tag="grp", align_bytes=64) for gp in range(2)]
+            lab = blk["label"]
+            blk["codes"] = [blk["pool"].tile([P, 512], U32, name=lab + "c", tag=lab + "c", align_bytes=64) for g in range(NG)]
+            blk["scales"] = [blk["pool"].tile([P, 512], U8, name=lab + "s", tag=lab + "s", align_bytes=64) for g in range(NG)]
+
+        def copies(blk, r):
+            for gp in range(2):
+                dst = blk["grouped"][gp][:].bitcast(F32).rearrange("p (g r i u) -> p g r i u", g=2, r=4, u=2)[:, :, r]
+                src = blk["banks"][(r, gp)][:].rearrange("p (g u i) -> p g i u", g=2, u=2)
+                if gp == 0:
                     nc.scalar.copy(out=dst, in_=src)
                 else:
                     nc.vector.tensor_copy(out=dst, in_=src)
-            c["grouped"] = grouped
 
-        def quantise(c):
-            codes = c["pool"].tile([P, 512], U32, name=c["label"] + "c", tag=c["label"] + "c", align_bytes=64)
-            scales = c["pool"].tile([P, 512], U8, name=c["label"] + "s", tag=c["label"] + "s", align_bytes=64)
-            nc.vector.quantize_mx(out=codes[:].bitcast(c["fmt"]), scales=scales[:], in_=c["grouped"][:])
-            c["codes"] = codes
-            c["scales"] = scales
+        def quantise(blk, g, c0, ncols):
+            lo = (g % 2) * 2048 + 4 * c0
+            nc.vector.quantize_mx(
+                out=blk["codes"][g][:, c0 : c0 + ncols].bitcast(blk["fmt"]),
+                scales=blk["scales"][g][:, c0 : c0 + ncols],
+                in_=blk["grouped"][g // 2][:, lo : lo + 4 * ncols],
+            )
 
-        def prepare(chunks):
-            for c in chunks:
-                transposes(c)
-            for c in chunks:
-                copies(c)
-            for c in chunks:
-                quantise(c)
+        def prepare_slice(blk, r):
+            transposes(blk, r)
+            copies(blk, r)
+            for g in range(NG):
+                quantise(blk, g, r * P, P)
 
-        def mx_pass(bank, gc, wc, bt, start, stop):
+        def prepare_block(blk):
+            open_block(blk)
+            for r in range(4):
+                transposes(blk, r)
+            for r in range(4):
+                copies(blk, r)
+            for g in range(NG):
+                quantise(blk, g, 0, 512)
+
+        def mx_pass(bank, wblk, bt, g):
             cols = slice(bt * P, (bt + 1) * P)
             nc.tensor.matmul_mx(
                 out=bank[:],
-                lhsT=gc["codes"][:, cols].bitcast(E5X4),
-                lhsT_scale=gc["scales"][:, cols],
-                rhs=wc["codes"][:].bitcast(E4X4),
-                rhs_scale=wc["scales"][:],
-                start=start,
-                stop=stop,
+                lhsT=gblk["codes"][g][:, cols].bitcast(E5X4),
+                lhsT_scale=gblk["scales"][g][:, cols],
+                rhs=wblk["codes"][g][:].bitcast(E4X4),
+                rhs_scale=wblk["scales"][g][:],
+                start=(g == 0),
+                stop=(g == NG - 1),
             )
 
         stages = {}
@@ -132,64 +139,51 @@ def tile_applypolicymap_kernel(tc, x, fc1, grad_out, out):
                     in_=stage,
                 )
 
-        def mx_run(gcs, wcs, j, bt0):
-            banks = []
-            for bt in (bt0, bt0 + 1):
-                bank = psum.tile([P, 512], F32, name="bank", tag="bank")
-                for g in range(NG):
-                    mx_pass(bank, gcs[g], wcs[g], bt, g == 0, g == NG - 1)
-                banks.append(bank)
-            drain(banks, j, bt0)
+        def multiply(j):
+            for bt0 in (0, 2):
+                banks = []
+                for bt in (bt0, bt0 + 1):
+                    bank = psum.tile([P, 512], F32, name="bank", tag="bank")
+                    for g in range(NG):
+                        mx_pass(bank, wblks[j], bt, g)
+                    banks.append(bank)
+                drain(banks, j, bt0)
 
-        g_raw = []
-        w0_raw = []
-        for g in range(NG):
-            g_raw.append(load(quarter, grad_out, 0, 512 * g, 512, "q"))
-            w0_raw.append(load(quarter, fc1, 0, 512 * g, 512, "q"))
-        w_chunks = {}
-        for j in (1, 2):
-            cs = []
-            for hk in range(2):
-                raw = load(half, fc1, 512 * j, 1024 * hk, 1024, "h")
-                cs.extend([chunk(raw, 1024, gl, E4X4, wq, "w") for gl in range(2)])
-            w_chunks[j] = cs
+        gblk = new_block(grad_out, 0, E5X4, gq, "g")
+        wblks = [new_block(fc1, 512 * j, E4X4, wq, "w") for j in range(NJ)]
 
-        def load_whole(j):
-            raw = load(whole, fc1, 512 * j, 0, K, "wj")
-            w_chunks[j] = [chunk(raw, K, g, E4X4, wq, "w") for g in range(NG)]
+        for r in range(4):
+            load(gblk, slices, r, 1, "sl")
+        for r in range(4):
+            load(wblks[0], slices, r, 1, "sl")
+        pending = [(j, h) for j in range(1, NJ) for h in range(2)]
 
-        load_whole(3)
-        load_whole(4)
+        issued = {"n": 0}
 
-        g_chunks = [chunk(g_raw[g], 512, 0, E5X4, gq, "g") for g in range(NG)]
-        w_chunks[0] = [chunk(w0_raw[g], 512, 0, E4X4, wq, "w") for g in range(NG)]
+        def more_loads(n):
+            for (j, h) in pending[issued["n"] : issued["n"] + n]:
+                load(wblks[j], halves, 2 * h, 2, "hf")
+            issued["n"] = issued["n"] + n
+
+        more_loads(8)
+
+        open_block(gblk)
+        for r in range(4):
+            prepare_slice(gblk, r)
+        open_block(wblks[0])
+        for r in range(4):
+            prepare_slice(wblks[0], r)
         banks0 = [psum.tile([P, 512], F32, name="bank", tag="bank") for bt in range(4)]
-
-        def head_run(g):
-            for bt in range(4):
-                mx_pass(banks0[bt], g_chunks[g], w_chunks[0][g], bt, g == 0, g == NG - 1)
-
         for g in range(NG):
-            prepare([g_chunks[g]])
-            prepare([w_chunks[0][g]])
-            if g >= 1:
-                head_run(g - 1)
-        prepare(w_chunks[1][0:2])
-        head_run(NG - 1)
+            for bt in range(4):
+                mx_pass(banks0[bt], wblks[0], bt, g)
         drain(banks0[0:2], 0, 0)
         drain(banks0[2:4], 0, 2)
-        prepare(w_chunks[1][2:4])
+        prepare_block(wblks[1])
+        more_loads(2)
 
         for j in range(1, NJ):
-            last = j == NJ - 1
-            long_runs = j >= 3
-            if not last:
-                prepare(w_chunks[j + 1] if long_runs else w_chunks[j + 1][0:2])
-            mx_run(g_chunks, w_chunks[j], j, 0)
-            if not last and not long_runs:
-                prepare(w_chunks[j + 1][2:4])
-            mx_run(g_chunks, w_chunks[j], j, 2)
-            if j % 2 == 1:
-                for jn in (j + 4, j + 5):
-                    if jn < NJ:
-                        load_whole(jn)
+            if j + 1 < NJ:
+                prepare_block(wblks[j + 1])
+                more_loads(2)
+            multiply(j)

@@ -14,7 +14,6 @@ P = 128
 B = 512
 IN_DIM = 5120
 K = 2048
-KW = K // 2
 NJ = IN_DIM // 512
 NG = K // 512
 
@@ -28,92 +27,96 @@ def tile_applypolicymap_kernel(tc, x, fc1, grad_out, out):
 
     with ExitStack() as ctx:
         const = ctx.enter_context(tc.tile_pool(name="const", bufs=1))
-        slices = ctx.enter_context(tc.tile_pool(name="slices", bufs=8))
-        halves = ctx.enter_context(tc.tile_pool(name="halves", bufs=8))
-        gpool = ctx.enter_context(tc.tile_pool(name="grouped", bufs=4))
+        quarter = ctx.enter_context(tc.tile_pool(name="quarter", bufs=8))
+        half = ctx.enter_context(tc.tile_pool(name="half", bufs=4))
+        whole = ctx.enter_context(tc.tile_pool(name="whole", bufs=4))
+        gpool = ctx.enter_context(tc.tile_pool(name="grouped", bufs=5))
         wq = ctx.enter_context(tc.tile_pool(name="wq", bufs=10))
         gq = ctx.enter_context(tc.tile_pool(name="gq", bufs=4))
-        spool = ctx.enter_context(tc.tile_pool(name="stage", bufs=7))
+        spool = ctx.enter_context(tc.tile_pool(name="stage", bufs=5))
         psum = ctx.enter_context(tc.psum_pool(name="psum", bufs=8))
         ctx.enter_context(tc.manual_schedule())
 
         ident = const.tile([P, P], F32, name="ident")
         make_identity(nc, ident[:])
 
-        def new_block(src, row0, fmt, pool, label):
+        ones = const.tile([P, 512], BF16, name="ones")
+        nc.vector.memset(ones[:], 1.0)
+        idle_bank = psum.tile([P, 512], F32, name="bank", tag="bank")
+
+        def warm_up(n):
+            for i in range(n):
+                nc.tensor.matmul(out=idle_bank[:], lhsT=ones[:, 0:P], rhs=ones[:], start=True, stop=True)
+
+        warm_up(6)
+
+        def load(pool, src, row0, k0, klen, label):
+            raw = pool.tile([P, 4 * klen], BF16, name=label, tag=label)
+            nc.sync.dma_start(
+                out=raw[:].rearrange("p (r k) -> p r k", r=4),
+                in_=src[row0 : row0 + 512, k0 : k0 + klen].rearrange("(r p) k -> p r k", p=P),
+            )
+            return raw
+
+        def chunk(raw, klen, g_local, fmt, pool, label):
             return {
-                "rows": src[row0 : row0 + 512, :].rearrange("(r p) k -> p r k", p=P),
+                "words": raw[:].bitcast(F32),
+                "rstride": klen // 2,
+                "goff": 256 * g_local,
                 "fmt": fmt,
                 "pool": pool,
                 "label": label,
-                "words": {},
-                "banks": {},
             }
 
-        def load(blk, pool, r0, nr, label):
-            raw = pool.tile([P, nr * K], BF16, name=label, tag=label)
-            nc.sync.dma_start(out=raw[:].rearrange("p (r k) -> p r k", r=nr), in_=blk["rows"][:, r0 : r0 + nr, :])
-            for i in range(nr):
-                blk["words"][r0 + i] = raw[:].bitcast(F32)[:, i * KW : (i + 1) * KW]
-
-        def transposes(blk, r):
-            for gp in range(2):
+        def transposes(c):
+            banks = []
+            for h in range(2):
                 bank = psum.tile([P, 512], F32, name="bank", tag="bank")
-                for g2 in range(2):
+                for rr in range(2):
                     for u in range(2):
-                        off = (2 * gp + g2) * 256 + 128 * u
-                        col = (2 * g2 + u) * 128
-                        nc.tensor.transpose(bank[:, col : col + 128], blk["words"][r][:, off : off + 128], ident[:])
-                blk["banks"][(r, gp)] = bank
+                        off = (2 * h + rr) * c["rstride"] + c["goff"] + 128 * u
+                        col = (2 * rr + u) * 128
+                        nc.tensor.transpose(bank[:, col : col + 128], c["words"][:, off : off + 128], ident[:])
+                banks.append(bank)
+            c["banks"] = banks
 
-        def open_block(blk):
-            blk["grouped"] = [gpool.tile([P, 4096], BF16, name="grp", tag="grp", align_bytes=64) for gp in range(2)]
-            lab = blk["label"]
-            blk["codes"] = [blk["pool"].tile([P, 512], U32, name=lab + "c", tag=lab + "c", align_bytes=64) for g in range(NG)]
-            blk["scales"] = [blk["pool"].tile([P, 512], U8, name=lab + "s", tag=lab + "s", align_bytes=64) for g in range(NG)]
-
-        def copies(blk, r):
-            for gp in range(2):
-                dst = blk["grouped"][gp][:].bitcast(F32).rearrange("p (g r i u) -> p g r i u", g=2, r=4, u=2)[:, :, r]
-                src = blk["banks"][(r, gp)][:].rearrange("p (g u i) -> p g i u", g=2, u=2)
-                if gp == 0:
+        def copies(c):
+            grouped = gpool.tile([P, 2048], BF16, name="grp", tag="grp", align_bytes=64)
+            gw = grouped[:].bitcast(F32)
+            for h in range(2):
+                dst = gw[:, 512 * h : 512 * h + 512].rearrange("p (r i u) -> p r i u", r=2, u=2)
+                src = c["banks"][h][:].rearrange("p (r u i) -> p r i u", r=2, u=2)
+                if h == 0:
                     nc.scalar.copy(out=dst, in_=src)
                 else:
                     nc.vector.tensor_copy(out=dst, in_=src)
+            c["grouped"] = grouped
 
-        def quantise(blk, g, c0, ncols):
-            lo = (g % 2) * 2048 + 4 * c0
-            nc.vector.quantize_mx(
-                out=blk["codes"][g][:, c0 : c0 + ncols].bitcast(blk["fmt"]),
-                scales=blk["scales"][g][:, c0 : c0 + ncols],
-                in_=blk["grouped"][g // 2][:, lo : lo + 4 * ncols],
-            )
+        def quantise(c):
+            codes = c["pool"].tile([P, 512], U32, name=c["label"] + "c", tag=c["label"] + "c", align_bytes=64)
+            scales = c["pool"].tile([P, 512], U8, name=c["label"] + "s", tag=c["label"] + "s", align_bytes=64)
+            nc.vector.quantize_mx(out=codes[:].bitcast(c["fmt"]), scales=scales[:], in_=c["grouped"][:])
+            c["codes"] = codes
+            c["scales"] = scales
 
-        def prepare_slice(blk, r):
-            transposes(blk, r)
-            copies(blk, r)
-            for g in range(NG):
-                quantise(blk, g, r * P, P)
+        def prepare(chunks):
+            for c in chunks:
+                transposes(c)
+            for c in chunks:
+                copies(c)
+            for c in chunks:
+                quantise(c)
 
-        def prepare_block(blk):
-            open_block(blk)
-            for r in range(4):
-                transposes(blk, r)
-            for r in range(4):
-                copies(blk, r)
-            for g in range(NG):
-                quantise(blk, g, 0, 512)
-
-        def mx_pass(bank, wblk, bt, g):
+        def mx_pass(bank, gc, wc, bt, start, stop):
             cols = slice(bt * P, (bt + 1) * P)
             nc.tensor.matmul_mx(
                 out=bank[:],
-                lhsT=gblk["codes"][g][:, cols].bitcast(E5X4),
-                lhsT_scale=gblk["scales"][g][:, cols],
-                rhs=wblk["codes"][g][:].bitcast(E4X4),
-                rhs_scale=wblk["scales"][g][:],
-                start=(g == 0),
-                stop=(g == NG - 1),
+                lhsT=gc["codes"][:, cols].bitcast(E5X4),
+                lhsT_scale=gc["scales"][:, cols],
+                rhs=wc["codes"][:].bitcast(E4X4),
+                rhs_scale=wc["scales"][:],
+                start=start,
+                stop=stop,
             )
 
         stages = {}
@@ -128,10 +131,14 @@ def tile_applypolicymap_kernel(tc, x, fc1, grad_out, out):
             stage = stages[key][:].rearrange("p (b c) -> p b c", b=2)
             last = j == NJ - 1 and bt0 == 2
             for i in range(2):
-                nc.scalar.copy(out=stage[:, i, c0 : c0 + 512], in_=banks[i][:])
-                if last:
-                    r0 = (bt0 + i) * P
-                    nc.sync.dma_start(out=out2d[r0 : r0 + P, 512 * j : 512 * j + 512], in_=stage[:, i, :])
+                pieces = 2 if last and i == 1 else 1
+                w = 512 // pieces
+                for h in range(pieces):
+                    nc.scalar.copy(out=stage[:, i, c0 + h * w : c0 + (h + 1) * w], in_=banks[i][:, h * w : (h + 1) * w])
+                    if last:
+                        r0 = (bt0 + i) * P
+                        col = 512 * j + h * w
+                        nc.sync.dma_start(out=out2d[r0 : r0 + P, col : col + w], in_=stage[:, i, h * w : (h + 1) * w])
             if not last and (not paired or j % 2 == 1):
                 col0 = 512 * j + 512 - width
                 nc.sync.dma_start(
@@ -139,51 +146,70 @@ def tile_applypolicymap_kernel(tc, x, fc1, grad_out, out):
                     in_=stage,
                 )
 
-        def multiply(j):
-            for bt0 in (0, 2):
-                banks = []
-                for bt in (bt0, bt0 + 1):
-                    bank = psum.tile([P, 512], F32, name="bank", tag="bank")
-                    for g in range(NG):
-                        mx_pass(bank, wblks[j], bt, g)
-                    banks.append(bank)
-                drain(banks, j, bt0)
+        def mx_run(gcs, wcs, j, bt0):
+            banks = []
+            for bt in (bt0, bt0 + 1):
+                bank = psum.tile([P, 512], F32, name="bank", tag="bank")
+                for g in range(NG):
+                    mx_pass(bank, gcs[g], wcs[g], bt, g == 0, g == NG - 1)
+                banks.append(bank)
+            drain(banks, j, bt0)
 
-        gblk = new_block(grad_out, 0, E5X4, gq, "g")
-        wblks = [new_block(fc1, 512 * j, E4X4, wq, "w") for j in range(NJ)]
-
-        for r in range(4):
-            load(gblk, slices, r, 1, "sl")
-        for r in range(4):
-            load(wblks[0], slices, r, 1, "sl")
-        pending = [(j, h) for j in range(1, NJ) for h in range(2)]
-
-        issued = {"n": 0}
-
-        def more_loads(n):
-            for (j, h) in pending[issued["n"] : issued["n"] + n]:
-                load(wblks[j], halves, 2 * h, 2, "hf")
-            issued["n"] = issued["n"] + n
-
-        more_loads(8)
-
-        open_block(gblk)
-        for r in range(4):
-            prepare_slice(gblk, r)
-        open_block(wblks[0])
-        for r in range(4):
-            prepare_slice(wblks[0], r)
-        banks0 = [psum.tile([P, 512], F32, name="bank", tag="bank") for bt in range(4)]
+        g_raw = []
+        w0_raw = []
         for g in range(NG):
+            g_raw.append(load(quarter, grad_out, 0, 512 * g, 512, "q"))
+            w0_raw.append(load(quarter, fc1, 0, 512 * g, 512, "q"))
+        w_chunks = {}
+        for j in (1, 2):
+            cs = []
+            for hk in range(2):
+                raw = load(half, fc1, 512 * j, 1024 * hk, 1024, "h")
+                cs.extend([chunk(raw, 1024, gl, E4X4, wq, "w") for gl in range(2)])
+            w_chunks[j] = cs
+
+        def load_whole(j):
+            raw = load(whole, fc1, 512 * j, 0, K, "wj")
+            w_chunks[j] = [chunk(raw, K, g, E4X4, wq, "w") for g in range(NG)]
+
+        load_whole(3)
+        load_whole(4)
+
+        g_chunks = [chunk(g_raw[g], 512, 0, E5X4, gq, "g") for g in range(NG)]
+        w_chunks[0] = [chunk(w0_raw[g], 512, 0, E4X4, wq, "w") for g in range(NG)]
+        banks0 = []
+
+        def head_run(g):
+            if g == 0:
+                banks0.extend([psum.tile([P, 512], F32, name="bank", tag="bank") for bt in range(4)])
             for bt in range(4):
-                mx_pass(banks0[bt], wblks[0], bt, g)
+                mx_pass(banks0[bt], g_chunks[g], w_chunks[0][g], bt, g == 0, g == NG - 1)
+
+        for g in range(NG):
+            prepare([g_chunks[g]])
+            if g <= 1:
+                warm_up(1)
+            prepare([w_chunks[0][g]])
+            if g == 0:
+                warm_up(1)
+            if g >= 1:
+                head_run(g - 1)
+        prepare(w_chunks[1][0:2])
+        head_run(NG - 1)
         drain(banks0[0:2], 0, 0)
         drain(banks0[2:4], 0, 2)
-        prepare_block(wblks[1])
-        more_loads(2)
+        prepare(w_chunks[1][2:4])
 
         for j in range(1, NJ):
-            if j + 1 < NJ:
-                prepare_block(wblks[j + 1])
-                more_loads(2)
-            multiply(j)
+            last = j == NJ - 1
+            long_runs = j >= 3
+            if not last:
+                prepare(w_chunks[j + 1] if long_runs else w_chunks[j + 1][0:2])
+            mx_run(g_chunks, w_chunks[j], j, 0)
+            if not last and not long_runs:
+                prepare(w_chunks[j + 1][2:4])
+            mx_run(g_chunks, w_chunks[j], j, 2)
+            if j % 2 == 1:
+                for jn in (j + 4, j + 5):
+                    if jn < NJ:
+                        load_whole(jn)

from contextlib import ExitStack

import concourse.mybir as mybir
from concourse.masks import make_identity

F32 = mybir.dt.float32
BF16 = mybir.dt.bfloat16
U32 = mybir.dt.uint32
U8 = mybir.dt.uint8
E4X4 = mybir.dt.float8_e4m3fn_x4
E5X4 = mybir.dt.float8_e5m2_x4

P = 128
B = 512
IN_DIM = 5120
K = 2048
NJ = IN_DIM // 512
NG = K // 512

FLOPS = 2 * B * IN_DIM * K
BYTES = IN_DIM * K * 2 + B * K * 2 + B * IN_DIM * 4


def tile_applypolicymap_kernel(tc, x, fc1, grad_out, out):
    nc = tc.nc
    out2d = out.rearrange("b c h w -> b (c h w)")

    with ExitStack() as ctx:
        const = ctx.enter_context(tc.tile_pool(name="const", bufs=1))
        quarter = ctx.enter_context(tc.tile_pool(name="quarter", bufs=8))
        half = ctx.enter_context(tc.tile_pool(name="half", bufs=4))
        whole = ctx.enter_context(tc.tile_pool(name="whole", bufs=4))
        gpool = ctx.enter_context(tc.tile_pool(name="grouped", bufs=5))
        wq = ctx.enter_context(tc.tile_pool(name="wq", bufs=10))
        gq = ctx.enter_context(tc.tile_pool(name="gq", bufs=4))
        spool = ctx.enter_context(tc.tile_pool(name="stage", bufs=5))
        psum = ctx.enter_context(tc.psum_pool(name="psum", bufs=8))
        ctx.enter_context(tc.manual_schedule())

        ident = const.tile([P, P], F32, name="ident")
        make_identity(nc, ident[:])

        ones = const.tile([P, 512], BF16, name="ones")
        nc.vector.memset(ones[:], 1.0)
        idle_bank = psum.tile([P, 512], F32, name="bank", tag="bank")

        def warm_up(n):
            for i in range(n):
                nc.tensor.matmul(out=idle_bank[:], lhsT=ones[:, 0:P], rhs=ones[:], start=True, stop=True)

        warm_up(6)

        def load(pool, src, row0, k0, klen, label):
            raw = pool.tile([P, 4 * klen], BF16, name=label, tag=label)
            nc.sync.dma_start(
                out=raw[:].rearrange("p (r k) -> p r k", r=4),
                in_=src[row0 : row0 + 512, k0 : k0 + klen].rearrange("(r p) k -> p r k", p=P),
            )
            return raw

        def chunk(raw, klen, g_local, fmt, pool, label):
            return {
                "words": raw[:].bitcast(F32),
                "rstride": klen // 2,
                "goff": 256 * g_local,
                "fmt": fmt,
                "pool": pool,
                "label": label,
            }

        def transposes(c):
            banks = []
            for h in range(2):
                bank = psum.tile([P, 512], F32, name="bank", tag="bank")
                for rr in range(2):
                    for u in range(2):
                        off = (2 * h + rr) * c["rstride"] + c["goff"] + 128 * u
                        col = (2 * rr + u) * 128
                        nc.tensor.transpose(bank[:, col : col + 128], c["words"][:, off : off + 128], ident[:])
                banks.append(bank)
            c["banks"] = banks

        def copies(c):
            grouped = gpool.tile([P, 2048], BF16, name="grp", tag="grp", align_bytes=64)
            gw = grouped[:].bitcast(F32)
            for h in range(2):
                dst = gw[:, 512 * h : 512 * h + 512].rearrange("p (r i u) -> p r i u", r=2, u=2)
                src = c["banks"][h][:].rearrange("p (r u i) -> p r i u", r=2, u=2)
                if h == 0:
                    nc.scalar.copy(out=dst, in_=src)
                else:
                    nc.vector.tensor_copy(out=dst, in_=src)
            c["grouped"] = grouped

        def quantise(c):
            codes = c["pool"].tile([P, 512], U32, name=c["label"] + "c", tag=c["label"] + "c", align_bytes=64)
            scales = c["pool"].tile([P, 512], U8, name=c["label"] + "s", tag=c["label"] + "s", align_bytes=64)
            nc.vector.quantize_mx(out=codes[:].bitcast(c["fmt"]), scales=scales[:], in_=c["grouped"][:])
            c["codes"] = codes
            c["scales"] = scales

        def prepare(chunks):
            for c in chunks:
                transposes(c)
            for c in chunks:
                copies(c)
            for c in chunks:
                quantise(c)

        def mx_pass(bank, gc, wc, bt, start, stop):
            cols = slice(bt * P, (bt + 1) * P)
            nc.tensor.matmul_mx(
                out=bank[:],
                lhsT=gc["codes"][:, cols].bitcast(E5X4),
                lhsT_scale=gc["scales"][:, cols],
                rhs=wc["codes"][:].bitcast(E4X4),
                rhs_scale=wc["scales"][:],
                start=start,
                stop=stop,
            )

        stages = {}

        def drain(banks, j, bt0):
            paired = j < NJ - 2
            width = 1024 if paired else 512
            c0 = 512 * (j % 2) if paired else 0
            key = (j // 2 if paired else j + NJ, bt0)
            if key not in stages:
                stages[key] = spool.tile([P, 2 * width], F32, name="st", tag="st")
            stage = stages[key][:].rearrange("p (b c) -> p b c", b=2)
            last = j == NJ - 1 and bt0 == 2
            for i in range(2):
                pieces = 2 if last and i == 1 else 1
                w = 512 // pieces
                for h in range(pieces):
                    nc.scalar.copy(out=stage[:, i, c0 + h * w : c0 + (h + 1) * w], in_=banks[i][:, h * w : (h + 1) * w])
                    if last:
                        r0 = (bt0 + i) * P
                        col = 512 * j + h * w
                        nc.sync.dma_start(out=out2d[r0 : r0 + P, col : col + w], in_=stage[:, i, h * w : (h + 1) * w])
            if not last and (not paired or j % 2 == 1):
                col0 = 512 * j + 512 - width
                nc.sync.dma_start(
                    out=out2d[bt0 * P : (bt0 + 2) * P, col0 : col0 + width].rearrange("(b p) c -> p b c", p=P),
                    in_=stage,
                )

        def mx_run(gcs, wcs, j, bt0):
            banks = []
            for bt in (bt0, bt0 + 1):
                bank = psum.tile([P, 512], F32, name="bank", tag="bank")
                for g in range(NG):
                    mx_pass(bank, gcs[g], wcs[g], bt, g == 0, g == NG - 1)
                banks.append(bank)
            drain(banks, j, bt0)

        g_raw = []
        w0_raw = []
        for g in range(NG):
            g_raw.append(load(quarter, grad_out, 0, 512 * g, 512, "q"))
            w0_raw.append(load(quarter, fc1, 0, 512 * g, 512, "q"))
        w_chunks = {}
        for j in (1, 2):
            cs = []
            for hk in range(2):
                raw = load(half, fc1, 512 * j, 1024 * hk, 1024, "h")
                cs.extend([chunk(raw, 1024, gl, E4X4, wq, "w") for gl in range(2)])
            w_chunks[j] = cs

        def load_whole(j):
            raw = load(whole, fc1, 512 * j, 0, K, "wj")
            w_chunks[j] = [chunk(raw, K, g, E4X4, wq, "w") for g in range(NG)]

        load_whole(3)
        load_whole(4)

        g_chunks = [chunk(g_raw[g], 512, 0, E5X4, gq, "g") for g in range(NG)]
        w_chunks[0] = [chunk(w0_raw[g], 512, 0, E4X4, wq, "w") for g in range(NG)]
        banks0 = []

        def head_run(g):
            if g == 0:
                banks0.extend([psum.tile([P, 512], F32, name="bank", tag="bank") for bt in range(4)])
            for bt in range(4):
                mx_pass(banks0[bt], g_chunks[g], w_chunks[0][g], bt, g == 0, g == NG - 1)

        for g in range(NG):
            prepare([g_chunks[g]])
            if g <= 1:
                warm_up(1)
            prepare([w_chunks[0][g]])
            if g == 0:
                warm_up(1)
            if g >= 1:
                head_run(g - 1)
        prepare(w_chunks[1][0:2])
        head_run(NG - 1)
        drain(banks0[0:2], 0, 0)
        drain(banks0[2:4], 0, 2)
        prepare(w_chunks[1][2:4])

        for j in range(1, NJ):
            last = j == NJ - 1
            long_runs = j >= 3
            if not last:
                prepare(w_chunks[j + 1] if long_runs else w_chunks[j + 1][0:2])
            mx_run(g_chunks, w_chunks[j], j, 0)
            if not last and not long_runs:
                prepare(w_chunks[j + 1][2:4])
            mx_run(g_chunks, w_chunks[j], j, 2)
            if j % 2 == 1:
                for jn in (j + 4, j + 5):
                    if jn < NJ:
                        load_whole(jn)
